import numpy as np
import ml_dtypes


def mxq(x, axis, fmt="e4m3"):
    dtype, down = {"e4m3": (ml_dtypes.float8_e4m3fn, 7), "e5m2": (ml_dtypes.float8_e5m2, 14)}[fmt]
    v = np.moveaxis(np.asarray(x, np.float32).astype(ml_dtypes.bfloat16).astype(np.float64), axis, -1)
    blocks = v.reshape(v.shape[:-1] + (-1, 32))
    amax = np.abs(blocks).max(-1, keepdims=True)
    byte = np.maximum(np.where(amax > 0, np.frexp(amax)[1] - 1 + 127, 0) - down, 1)
    scale = np.exp2(byte - 127.0)
    codes = (blocks / scale).astype(np.float32).astype(dtype).astype(np.float64)
    return np.moveaxis((codes * scale).reshape(v.shape), -1, axis)


WIDE = False


def mx_kscale(k):
    if not WIDE:
        return np.ones(k)
    levels = np.array([10, -10, 5, -5, 0])
    if k % 512:
        return np.exp2(np.random.permutation(np.resize(levels, k // 32))).repeat(32)
    a = np.empty((k // 512, 16))
    for p in range(k // 512):
        a[p, :8] = np.random.permutation(np.resize(levels, 8))
        for g in range(8):
            far = levels[np.abs(levels - a[p, g]) >= 10]
            a[p, g + 8] = far[np.random.randint(len(far))]
    return np.exp2(a.ravel()).repeat(32)


BF16 = ml_dtypes.bfloat16


def bf(x):
    return np.asarray(x, np.float32).astype(BF16)


def f64(x):
    return np.asarray(x).astype(np.float64)


B, C, N, T, Q = 4, 128, 512, 8, 4


def setup_inputs():
    s = mx_kscale(N)
    a = 2.0 / np.sqrt(N)
    return {"x": bf(np.random.standard_normal((B, C, N, T)) * s[:, None]),
            "Ar": bf(np.random.uniform(0.0, 1.0, (N, N)) * a / s),
            "Ai": bf(np.random.uniform(0.0, 1.0, (N, N)) * a / s),
            "Aj": bf(np.random.uniform(0.0, 1.0, (N, N)) * a / s),
            "Ak": bf(np.random.uniform(0.0, 1.0, (N, N)) * a / s)}


def reference(x, Ar, Ai, Aj, Ak):
    xq = mxq(f64(x), 2, "e4m3")
    Yr = mxq(f64(Ar), 1, "e4m3") @ xq
    Yi = mxq(f64(Ai), 1, "e4m3") @ xq
    Yj = mxq(f64(Aj), 1, "e4m3") @ xq
    Yk = mxq(f64(Ak), 1, "e4m3") @ xq
    Yr_r, Yr_i, Yr_j, Yr_k = np.split(Yr, Q, axis=1)
    Yi_r, Yi_i, Yi_j, Yi_k = np.split(Yi, Q, axis=1)
    Yj_r, Yj_i, Yj_j, Yj_k = np.split(Yj, Q, axis=1)
    Yk_r, Yk_i, Yk_j, Yk_k = np.split(Yk, Q, axis=1)
    out_r = Yr_r - Yi_i - Yj_j - Yk_k
    out_i = Yr_i + Yi_r + Yj_k - Yk_j
    out_j = Yr_j - Yi_k + Yj_r + Yk_i
    out_k = Yr_k + Yi_j - Yj_i + Yk_r
    return np.concatenate([out_r, out_i, out_j, out_k], axis=1)

@@ -1,0 +1,224 @@
+from contextlib import ExitStack
+
+import concourse.mybir as mybir
+from concourse.masks import make_identity
+
+F32 = mybir.dt.float32
+BF16 = mybir.dt.bfloat16
+U32 = mybir.dt.uint32
+U8 = mybir.dt.uint8
+FP8X4 = mybir.dt.float8_e4m3fn_x4
+
+B, C, N, T, Q = 4, 128, 512, 8, 4
+P = 128
+PACK = 4
+GROUP = C // Q
+N_TILES = N // P
+T_PAIRS = T // 2
+T_BANK = 4
+T_HALVES = T // T_BANK
+BANK = 512
+PSUM_BANKS = 8
+
+SIGN = (
+    (+1, -1, -1, -1),
+    (+1, +1, +1, -1),
+    (+1, -1, +1, +1),
+    (+1, +1, -1, +1),
+)
+SLOTS = 2 * Q - 1
+SLOT_RUNS = ((0, 4), (4, 2), (6, 1))
+
+FLOPS = 2 * Q * N * N * B * C * T
+
+
+def slot_of(g, a):
+    return a if SIGN[g][a] > 0 else Q - 1 + a
+
+
+def tile_nconv_pa_t_kernel(tc, x, Ar, Ai, Aj, Ak, out):
+    nc = tc.nc
+    adjacency = (Ar, Ai, Aj, Ak)
+
+    with ExitStack() as stack:
+        keep = stack.enter_context(tc.tile_pool(name="keep", bufs=1))
+        a_stage = stack.enter_context(tc.tile_pool(name="a_stage", bufs=2))
+        o_stage = stack.enter_context(tc.tile_pool(name="o_stage", bufs=2))
+        psum = stack.enter_context(tc.psum_pool(name="psum", bufs=PSUM_BANKS))
+        stack.enter_context(tc.manual_schedule())
+
+        ident = keep.tile([P, P], F32)
+        make_identity(nc, ident[:])
+
+        a_rows = [
+            [keep.tile([P, N], BF16, name="a_rows_%d_%d" % (nt, a)) for a in range(Q)]
+            for nt in range(N_TILES)
+        ]
+
+        def load_adjacency(nt):
+            for a in range(Q):
+                nc.sync.dma_start(
+                    out=a_rows[nt][a][:], in_=adjacency[a][nt * P : (nt + 1) * P, :]
+                )
+
+        load_adjacency(0)
+        x_raw = []
+        for g in range(Q):
+            raw = keep.tile([P, N * T], BF16, name="x_raw_%d" % g)
+            for b in range(B):
+                nc.sync.dma_start(
+                    out=raw[b:P:B, :],
+                    in_=x[b, g * GROUP : (g + 1) * GROUP].rearrange("c m t -> c (m t)"),
+                )
+            x_raw.append(raw)
+        for nt in range(1, N_TILES):
+            load_adjacency(nt)
+
+        pair_width = 2 * P * PACK
+        x_grouped = [
+            keep.tile([P, T_PAIRS * pair_width], BF16, name="x_grouped_%d" % g, align_bytes=64)
+            for g in range(Q)
+        ]
+        x_codes = [
+            [
+                keep.tile([P, 2 * P], U32, name="x_codes_%d_%d" % (g, w), align_bytes=64)
+                for w in range(T_PAIRS)
+            ]
+            for g in range(Q)
+        ]
+        x_scales = [
+            [
+                keep.tile([P, 2 * P], U8, name="x_scales_%d_%d" % (g, w), align_bytes=64)
+                for w in range(T_PAIRS)
+            ]
+            for g in range(Q)
+        ]
+
+        def transpose_x(g, w):
+            words = x_raw[g][:].bitcast(F32).rearrange(
+                "p (q j w) -> p q j w", q=P, j=PACK, w=T_PAIRS
+            )
+            bank = psum.tile([P, BANK], F32, tag="bank")
+            for j in range(PACK):
+                nc.tensor.transpose(bank[:, j * P : (j + 1) * P], words[:, :, j, w], ident[:])
+            return bank
+
+        def regroup_x(copy, g, w, bank):
+            target = x_grouped[g][:, w * pair_width : (w + 1) * pair_width]
+            copy(
+                out=target.rearrange("p (s c j) -> p s c j", s=2, c=P, j=PACK),
+                in_=bank[:].bitcast(BF16).rearrange("p (j c s) -> p s c j", j=PACK, c=P, s=2),
+            )
+
+        def quantise_x(g, w):
+            nc.vector.quantize_mx(
+                out=x_codes[g][w][:].bitcast(FP8X4),
+                scales=x_scales[g][w][:],
+                in_=x_grouped[g][:, w * pair_width : (w + 1) * pair_width],
+            )
+
+        a_codes = [
+            keep.tile([P, SLOTS * P], U32, name="a_codes_%d" % nt, align_bytes=64)
+            for nt in range(N_TILES)
+        ]
+        a_scales = [
+            keep.tile([P, SLOTS * P], U8, name="a_scales_%d" % nt, align_bytes=64)
+            for nt in range(N_TILES)
+        ]
+
+        slot_width = P * PACK
+
+        def transpose_adjacency(nt):
+            grouped = a_stage.tile([P, SLOTS * slot_width], BF16, tag="grouped", align_bytes=64)
+            grouped_words = grouped[:].bitcast(F32).rearrange(
+                "p (s n u) -> p s n u", s=SLOTS, n=P, u=2
+            )
+            for pair in range(2):
+                bank = psum.tile([P, BANK], F32, tag="bank")
+                for i in range(2):
+                    words = a_rows[nt][2 * pair + i][:].bitcast(F32)
+                    for u in range(2):
+                        k = 2 * i + u
+                        nc.tensor.transpose(
+                            bank[:, k * P : (k + 1) * P], words[:, u : 2 * P : 2], ident[:]
+                        )
+                nc.scalar.copy(
+                    out=grouped_words[:, 2 * pair : 2 * pair + 2, :, :],
+                    in_=bank[:].rearrange("p (s u n) -> p s n u", s=2, u=2, n=P),
+                )
+            return grouped
+
+        def quantise_adjacency(nt, grouped):
+            nc.vector.tensor_scalar_mul(
+                out=grouped[:, Q * slot_width : SLOTS * slot_width],
+                in0=grouped[:, slot_width : Q * slot_width],
+                scalar1=-1.0,
+            )
+            for first, count in SLOT_RUNS:
+                nc.vector.quantize_mx(
+                    out=a_codes[nt][:, first * P : (first + count) * P].bitcast(FP8X4),
+                    scales=a_scales[nt][:, first * P : (first + count) * P],
+                    in_=grouped[:, first * slot_width : (first + count) * slot_width],
+                )
+
+        def multiply(nt, g, h, result):
+            acc = psum.tile([P, BANK], F32, tag="bank")
+            for tl in range(T_BANK):
+                t = h * T_BANK + tl
+                w, s = t // 2, t % 2
+                for a in range(Q):
+                    k = slot_of(g, a)
+                    nc.tensor.matmul_mx(
+                        out=acc[:, tl * P : (tl + 1) * P],
+                        lhsT=x_codes[g ^ a][w][:, s * P : (s + 1) * P].bitcast(FP8X4),
+                        lhsT_scale=x_scales[g ^ a][w][:, s * P : (s + 1) * P],
+                        rhs=a_codes[nt][:, k * P : (k + 1) * P].bitcast(FP8X4),
+                        rhs_scale=a_scales[nt][:, k * P : (k + 1) * P],
+                        start=(a == 0),
+                        stop=(a == Q - 1),
+                    )
+            copy = nc.scalar.copy if g % 2 == 0 else nc.vector.tensor_copy
+            copy(
+                out=result[:].rearrange("p (n t) -> p n t", n=P, t=T)[
+                    :, :, h * T_BANK : (h + 1) * T_BANK
+                ],
+                in_=acc[:].rearrange("p (t n) -> p n t", t=T_BANK, n=P),
+            )
+
+        def store(nt, g, result):
+            for b in range(B):
+                nc.sync.dma_start(
+                    out=out[
+                        b, g * GROUP : (g + 1) * GROUP, nt * P : (nt + 1) * P, :
+                    ].rearrange("c n t -> c (n t)"),
+                    in_=result[b:P:B, :],
+                )
+
+        quantise_adjacency(0, transpose_adjacency(0))
+        parked = []
+        for g in range(Q):
+            banks = [transpose_x(g, w) for w in range(T_PAIRS)]
+            regroup_x(nc.scalar.copy, g, 0, banks[0])
+            regroup_x(nc.vector.tensor_copy, g, 1, banks[1])
+            quantise_x(g, 0)
+            quantise_x(g, 1)
+            regroup_x(nc.scalar.copy, g, 2, banks[2])
+            if g > 0:
+                quantise_x(g - 1, 2)
+            parked.append(banks[3])
+        quantise_x(Q - 1, 2)
+        for g in range(Q):
+            regroup_x(nc.scalar.copy, g, 3, parked[g])
+            quantise_x(g, 3)
+
+        for nt in range(N_TILES):
+            results = [
+                o_stage.tile([P, P * T], F32, name="result_%d" % g) for g in range(Q)
+            ]
+            for h in range(T_HALVES):
+                for g in range(Q):
+                    multiply(nt, g, h, results[g])
+                    if h == T_HALVES - 1:
+                        store(nt, g, results[g])
+                if h == 0 and nt + 1 < N_TILES:
+                    quantise_adjacency(nt + 1, transpose_adjacency(nt + 1))

@@ -13,12 +13,10 @@ B, C, N, T, Q = 4, 128, 512, 8, 4
 P = 128
 PACK = 4
 GROUP = C // Q
-N_TILES = N // P
 T_PAIRS = T // 2
-T_BANK = 4
-T_HALVES = T // T_BANK
 BANK = 512
 PSUM_BANKS = 8
+LAST = Q - 1
 
 SIGN = (
     (+1, -1, -1, -1),
@@ -28,6 +26,8 @@ SIGN = (
 )
 SLOTS = 2 * Q - 1
 SLOT_RUNS = ((0, 4), (4, 2), (6, 1))
+
+RANGES = ((0, 1), (1, 2), (3, 1))
 
 FLOPS = 2 * Q * N * N * B * C * T
 
@@ -39,27 +39,26 @@ def slot_of(g, a):
 def tile_nconv_pa_t_kernel(tc, x, Ar, Ai, Aj, Ak, out):
     nc = tc.nc
     adjacency = (Ar, Ai, Aj, Ak)
+    by_scalar = nc.scalar.copy
+    by_vector = nc.vector.tensor_copy
 
     with ExitStack() as stack:
         keep = stack.enter_context(tc.tile_pool(name="keep", bufs=1))
-        a_stage = stack.enter_context(tc.tile_pool(name="a_stage", bufs=2))
-        o_stage = stack.enter_context(tc.tile_pool(name="o_stage", bufs=2))
+        narrow = stack.enter_context(tc.tile_pool(name="narrow", bufs=2))
+        wide = stack.enter_context(tc.tile_pool(name="wide", bufs=2))
         psum = stack.enter_context(tc.psum_pool(name="psum", bufs=PSUM_BANKS))
         stack.enter_context(tc.manual_schedule())
 
         ident = keep.tile([P, P], F32)
         make_identity(nc, ident[:])
 
-        a_rows = [
-            [keep.tile([P, N], BF16, name="a_rows_%d_%d" % (nt, a)) for a in range(Q)]
-            for nt in range(N_TILES)
-        ]
+        a_rows = {}
 
         def load_adjacency(nt):
             for a in range(Q):
-                nc.sync.dma_start(
-                    out=a_rows[nt][a][:], in_=adjacency[a][nt * P : (nt + 1) * P, :]
-                )
+                rows = keep.tile([P, N], BF16, name="a_rows_%d_%d" % (nt, a))
+                nc.sync.dma_start(out=rows[:], in_=adjacency[a][nt * P : (nt + 1) * P, :])
+                a_rows[nt, a] = rows
 
         load_adjacency(0)
         x_raw = []
@@ -71,28 +70,25 @@ def tile_nconv_pa_t_kernel(tc, x, Ar, Ai, Aj, Ak, out):
                     in_=x[b, g * GROUP : (g + 1) * GROUP].rearrange("c m t -> c (m t)"),
                 )
             x_raw.append(raw)
-        for nt in range(1, N_TILES):
+        for nt in range(1, N // P):
             load_adjacency(nt)
 
-        pair_width = 2 * P * PACK
-        x_grouped = [
-            keep.tile([P, T_PAIRS * pair_width], BF16, name="x_grouped_%d" % g, align_bytes=64)
-            for g in range(Q)
-        ]
-        x_codes = [
-            [
-                keep.tile([P, 2 * P], U32, name="x_codes_%d_%d" % (g, w), align_bytes=64)
-                for w in range(T_PAIRS)
-            ]
-            for g in range(Q)
-        ]
-        x_scales = [
-            [
-                keep.tile([P, 2 * P], U8, name="x_scales_%d_%d" % (g, w), align_bytes=64)
-                for w in range(T_PAIRS)
-            ]
-            for g in range(Q)
-        ]
+        step_width = P * PACK
+        x_grouped = {}
+        x_codes = {}
+        x_scales = {}
+        for g in range(Q):
+            for w in range(T_PAIRS):
+                x_grouped[g, w] = keep.tile(
+                    [P, 2 * step_width], BF16, name="x_grouped_%d_%d" % (g, w), align_bytes=64
+                )
+                x_codes[g, w] = keep.tile(
+                    [P, 2 * P], U32, name="x_codes_%d_%d" % (g, w), align_bytes=64
+                )
+                x_scales[g, w] = keep.tile(
+                    [P, 2 * P], U8, name="x_scales_%d_%d" % (g, w), align_bytes=64
+                )
+        x_banks = {}
 
         def transpose_x(g, w):
             words = x_raw[g][:].bitcast(F32).rearrange(
@@ -101,124 +97,192 @@ def tile_nconv_pa_t_kernel(tc, x, Ar, Ai, Aj, Ak, out):
             bank = psum.tile([P, BANK], F32, tag="bank")
             for j in range(PACK):
                 nc.tensor.transpose(bank[:, j * P : (j + 1) * P], words[:, :, j, w], ident[:])
-            return bank
+            x_banks[g, w] = bank
 
-        def regroup_x(copy, g, w, bank):
-            target = x_grouped[g][:, w * pair_width : (w + 1) * pair_width]
+        def regroup_x(copy, g, w, first=0, steps=2):
+            target = x_grouped[g, w][:, first * step_width : (first + steps) * step_width]
+            source = x_banks[g, w][:].bitcast(BF16).rearrange(
+                "p (j c s) -> p s c j", j=PACK, c=P, s=2
+            )
             copy(
-                out=target.rearrange("p (s c j) -> p s c j", s=2, c=P, j=PACK),
-                in_=bank[:].bitcast(BF16).rearrange("p (j c s) -> p s c j", j=PACK, c=P, s=2),
+                out=target.rearrange("p (s c j) -> p s c j", s=steps, c=P, j=PACK),
+                in_=source[:, first : first + steps, :, :],
             )
 
-        def quantise_x(g, w):
+        def quantise_x(g, w, first=0, steps=2):
             nc.vector.quantize_mx(
-                out=x_codes[g][w][:].bitcast(FP8X4),
-                scales=x_scales[g][w][:],
-                in_=x_grouped[g][:, w * pair_width : (w + 1) * pair_width],
+                out=x_codes[g, w][:, first * P : (first + steps) * P].bitcast(FP8X4),
+                scales=x_scales[g, w][:, first * P : (first + steps) * P],
+                in_=x_grouped[g, w][:, first * step_width : (first + steps) * step_width],
             )
 
-        a_codes = [
-            keep.tile([P, SLOTS * P], U32, name="a_codes_%d" % nt, align_bytes=64)
-            for nt in range(N_TILES)
-        ]
-        a_scales = [
-            keep.tile([P, SLOTS * P], U8, name="a_scales_%d" % nt, align_bytes=64)
-            for nt in range(N_TILES)
-        ]
+        a_grouped = []
+        a_codes = []
+        a_scales = []
+        for r in range(len(RANGES)):
+            columns = SLOTS * RANGES[r][1] * P
+            a_grouped.append(
+                keep.tile([P, PACK * columns], BF16, name="a_grouped_%d" % r, align_bytes=64)
+            )
+            a_codes.append(keep.tile([P, columns], U32, name="a_codes_%d" % r, align_bytes=64))
+            a_scales.append(keep.tile([P, columns], U8, name="a_scales_%d" % r, align_bytes=64))
 
-        slot_width = P * PACK
-
-        def transpose_adjacency(nt):
-            grouped = a_stage.tile([P, SLOTS * slot_width], BF16, tag="grouped", align_bytes=64)
-            grouped_words = grouped[:].bitcast(F32).rearrange(
-                "p (s n u) -> p s n u", s=SLOTS, n=P, u=2
+        def transpose_adjacency(r, i, copies):
+            first, tiles = RANGES[r]
+            grouped_words = a_grouped[r][:].bitcast(F32).rearrange(
+                "p (s i n u) -> p s i n u", s=SLOTS, i=tiles, n=P, u=2
             )
             for pair in range(2):
                 bank = psum.tile([P, BANK], F32, tag="bank")
-                for i in range(2):
-                    words = a_rows[nt][2 * pair + i][:].bitcast(F32)
-                    for u in range(2):
-                        k = 2 * i + u
-                        nc.tensor.transpose(
-                            bank[:, k * P : (k + 1) * P], words[:, u : 2 * P : 2], ident[:]
-                        )
-                nc.scalar.copy(
-                    out=grouped_words[:, 2 * pair : 2 * pair + 2, :, :],
+                for k in range(4):
+                    words = a_rows[first + i, 2 * pair + k // 2][:].bitcast(F32)
+                    nc.tensor.transpose(
+                        bank[:, k * P : (k + 1) * P], words[:, k % 2 : 2 * P : 2], ident[:]
+                    )
+                copies[pair](
+                    out=grouped_words[:, 2 * pair : 2 * pair + 2, i, :, :],
                     in_=bank[:].rearrange("p (s u n) -> p s n u", s=2, u=2, n=P),
                 )
-            return grouped
 
-        def quantise_adjacency(nt, grouped):
+        def negate_adjacency(r):
+            slot_width = RANGES[r][1] * P * PACK
             nc.vector.tensor_scalar_mul(
-                out=grouped[:, Q * slot_width : SLOTS * slot_width],
-                in0=grouped[:, slot_width : Q * slot_width],
+                out=a_grouped[r][:, Q * slot_width : SLOTS * slot_width],
+                in0=a_grouped[r][:, slot_width : Q * slot_width],
                 scalar1=-1.0,
             )
+
+        def quantise_adjacency(r):
+            columns = RANGES[r][1] * P
             for first, count in SLOT_RUNS:
+                span = slice(first * columns, (first + count) * columns)
                 nc.vector.quantize_mx(
-                    out=a_codes[nt][:, first * P : (first + count) * P].bitcast(FP8X4),
-                    scales=a_scales[nt][:, first * P : (first + count) * P],
-                    in_=grouped[:, first * slot_width : (first + count) * slot_width],
+                    out=a_codes[r][:, span].bitcast(FP8X4),
+                    scales=a_scales[r][:, span],
+                    in_=a_grouped[r][:, PACK * span.start : PACK * span.stop],
                 )
 
-        def multiply(nt, g, h, result):
-            acc = psum.tile([P, BANK], F32, tag="bank")
-            for tl in range(T_BANK):
-                t = h * T_BANK + tl
-                w, s = t // 2, t % 2
-                for a in range(Q):
-                    k = slot_of(g, a)
-                    nc.tensor.matmul_mx(
-                        out=acc[:, tl * P : (tl + 1) * P],
-                        lhsT=x_codes[g ^ a][w][:, s * P : (s + 1) * P].bitcast(FP8X4),
-                        lhsT_scale=x_scales[g ^ a][w][:, s * P : (s + 1) * P],
-                        rhs=a_codes[nt][:, k * P : (k + 1) * P].bitcast(FP8X4),
-                        rhs_scale=a_scales[nt][:, k * P : (k + 1) * P],
-                        start=(a == 0),
-                        stop=(a == Q - 1),
-                    )
-            copy = nc.scalar.copy if g % 2 == 0 else nc.vector.tensor_copy
-            copy(
-                out=result[:].rearrange("p (n t) -> p n t", n=P, t=T)[
-                    :, :, h * T_BANK : (h + 1) * T_BANK
-                ],
-                in_=acc[:].rearrange("p (t n) -> p n t", t=T_BANK, n=P),
-            )
+        def multiply(r, g, t, target):
+            columns = RANGES[r][1] * P
+            for a in range(Q):
+                s = slice((t % 2) * P, (t % 2 + 1) * P)
+                n = slice(slot_of(g, a) * columns, (slot_of(g, a) + 1) * columns)
+                nc.tensor.matmul_mx(
+                    out=target,
+                    lhsT=x_codes[g ^ a, t // 2][:, s].bitcast(FP8X4),
+                    lhsT_scale=x_scales[g ^ a, t // 2][:, s],
+                    rhs=a_codes[r][:, n].bitcast(FP8X4),
+                    rhs_scale=a_scales[r][:, n],
+                    start=(a == 0),
+                    stop=(a == Q - 1),
+                )
 
-        def store(nt, g, result):
+        def store(r, g, result):
+            first, tiles = RANGES[r]
             for b in range(B):
                 nc.sync.dma_start(
                     out=out[
-                        b, g * GROUP : (g + 1) * GROUP, nt * P : (nt + 1) * P, :
+                        b, g * GROUP : (g + 1) * GROUP, first * P : (first + tiles) * P, :
                     ].rearrange("c n t -> c (n t)"),
                     in_=result[b:P:B, :],
                 )
 
-        quantise_adjacency(0, transpose_adjacency(0))
-        parked = []
-        for g in range(Q):
-            banks = [transpose_x(g, w) for w in range(T_PAIRS)]
-            regroup_x(nc.scalar.copy, g, 0, banks[0])
-            regroup_x(nc.vector.tensor_copy, g, 1, banks[1])
+        def multiply_narrow(r, g, acc, steps):
+            for t in steps:
+                k = t % 4
+                multiply(r, g, t, acc[:, k * P : (k + 1) * P])
+
+        def unload_narrow(copy, h, acc, result):
+            copy(
+                out=result[:].rearrange("p (n t) -> p n t", n=P, t=T)[:, :, 4 * h : 4 * h + 4],
+                in_=acc[:].rearrange("p (t n) -> p n t", t=4, n=P),
+            )
+
+        def multiply_wide(r, g, w):
+            acc = psum.tile([P, BANK], F32, tag="bank")
+            for t in (2 * w, 2 * w + 1):
+                k = t % 2
+                multiply(r, g, t, acc[:, 2 * k * P : 2 * (k + 1) * P])
+            return acc
+
+        def permute_wide(h, staged, result):
+            nc.vector.tensor_copy(
+                out=result[:].rearrange("p (n t) -> p n t", n=2 * P, t=T)[
+                    :, :, 4 * h : 4 * h + 4
+                ],
+                in_=staged[:].rearrange("p (t n) -> p n t", t=T, n=2 * P)[
+                    :, :, 4 * h : 4 * h + 4
+                ],
+            )
+
+        transpose_adjacency(0, 0, (by_scalar, by_vector))
+        negate_adjacency(0)
+        quantise_adjacency(0)
+        for g in range(LAST):
+            for w in range(T_PAIRS):
+                transpose_x(g, w)
+            regroup_x(by_scalar, g, 0)
+            regroup_x(by_vector, g, 1)
             quantise_x(g, 0)
             quantise_x(g, 1)
-            regroup_x(nc.scalar.copy, g, 2, banks[2])
+            regroup_x(by_scalar, g, 2)
             if g > 0:
                 quantise_x(g - 1, 2)
-            parked.append(banks[3])
-        quantise_x(Q - 1, 2)
-        for g in range(Q):
-            regroup_x(nc.scalar.copy, g, 3, parked[g])
-            quantise_x(g, 3)
+        transpose_x(LAST, 0)
+        transpose_x(LAST, 1)
+        regroup_x(by_scalar, LAST, 0, 0, 1)
+        regroup_x(by_scalar, LAST, 0, 1, 1)
+        quantise_x(LAST, 0, 0, 1)
+        quantise_x(LAST, 0, 1, 1)
+        regroup_x(by_vector, LAST, 1)
+        quantise_x(LAST, 1)
+        quantise_x(LAST - 1, 2)
 
-        for nt in range(N_TILES):
-            results = [
-                o_stage.tile([P, P * T], F32, name="result_%d" % g) for g in range(Q)
-            ]
-            for h in range(T_HALVES):
-                for g in range(Q):
-                    multiply(nt, g, h, results[g])
-                    if h == T_HALVES - 1:
-                        store(nt, g, results[g])
-                if h == 0 and nt + 1 < N_TILES:
-                    quantise_adjacency(nt + 1, transpose_adjacency(nt + 1))
+        results = [narrow.tile([P, P * T], F32, name="result_%d" % g) for g in range(Q)]
+        accs = [psum.tile([P, BANK], F32, tag="bank", name="acc") for g in range(Q)]
+        for t in (0, 1):
+            for g in range(Q):
+                multiply_narrow(0, g, accs[g], (t,))
+        for g in range(LAST):
+            regroup_x(by_scalar, g, 3)
+            quantise_x(g, 3)
+        transpose_x(LAST, 2)
+        transpose_x(LAST, 3)
+        regroup_x(by_scalar, LAST, 2)
+        regroup_x(by_vector, LAST, 3)
+        quantise_x(LAST, 2)
+        quantise_x(LAST, 3)
+        for g in range(Q):
+            multiply_narrow(0, g, accs[g], (2, 3))
+            unload_narrow(by_vector if g % 2 else by_scalar, 0, accs[g], results[g])
+        for i in range(2):
+            transpose_adjacency(1, i, (by_scalar, by_vector))
+        negate_adjacency(1)
+        quantise_adjacency(1)
+        accs = [psum.tile([P, BANK], F32, tag="bank", name="acc") for g in range(Q)]
+        for g in range(Q):
+            multiply_narrow(0, g, accs[g], (4, 5, 6, 7))
+            unload_narrow(by_vector if g % 2 else by_scalar, 1, accs[g], results[g])
+            store(0, g, results[g])
+
+        for g in range(Q):
+            staged = wide.tile([P, 2 * P * T], F32, name="staged")
+            result = wide.tile([P, 2 * P * T], F32, name="result")
+            for w in range(T_PAIRS):
+                acc = multiply_wide(1, g, w)
+                by_scalar(out=staged[:, w * BANK : (w + 1) * BANK], in_=acc[:])
+                if w % 2 == 1:
+                    permute_wide(w // 2, staged, result)
+            store(1, g, result)
+            if g == 1:
+                transpose_adjacency(2, 0, (by_scalar, by_vector))
+                negate_adjacency(2)
+                quantise_adjacency(2)
+
+        for g in range(Q):
+            result = narrow.tile([P, P * T], F32, name="result_%d" % g)
+            for h in range(2):
+                acc = psum.tile([P, BANK], F32, tag="bank")
+                multiply_narrow(2, g, acc, range(4 * h, 4 * h + 4))
+                unload_narrow(by_vector if h else by_scalar, h, acc, result)
+            store(2, g, result)

@@ -27,7 +27,8 @@ SIGN = (
 SLOTS = 2 * Q - 1
 SLOT_RUNS = ((0, 4), (4, 2), (6, 1))
 
-RANGES = ((0, 1), (1, 2), (3, 1))
+RANGES = ((0, 1), (1, 1), (2, 2))
+SQUARE = 32
 
 FLOPS = 2 * Q * N * N * B * C * T
 
@@ -70,8 +71,21 @@ def tile_nconv_pa_t_kernel(tc, x, Ar, Ai, Aj, Ak, out):
                     in_=x[b, g * GROUP : (g + 1) * GROUP].rearrange("c m t -> c (m t)"),
                 )
             x_raw.append(raw)
-        for nt in range(1, N // P):
-            load_adjacency(nt)
+        load_adjacency(1)
+        block_width = 2 * N * RANGES[2][1]
+        a_blocks = keep.tile([P, 2 * block_width], BF16, name="a_blocks", align_bytes=64)
+        for a in range(Q):
+            rows = adjacency[a][RANGES[2][0] * P : (RANGES[2][0] + RANGES[2][1]) * P, :]
+            per_part = 2 * block_width // Q
+            for d in range(P // SQUARE):
+                nc.sync.dma_start(
+                    out=a_blocks[
+                        d * SQUARE : (d + 1) * SQUARE, a * per_part : (a + 1) * per_part
+                    ].rearrange("k (f i) -> k f i", i=4 * SQUARE),
+                    in_=rows[:, d * 4 * SQUARE : (d + 1) * 4 * SQUARE].rearrange(
+                        "(f k) i -> k f i", k=SQUARE
+                    ),
+                )
 
         step_width = P * PACK
         x_grouped = {}
@@ -144,6 +158,35 @@ def tile_nconv_pa_t_kernel(tc, x, Ar, Ai, Aj, Ak, out):
                     in_=bank[:].rearrange("p (s u n) -> p s n u", s=2, u=2, n=P),
                 )
 
+        half_words = block_width // 2
+        a_split = [
+            keep.tile([P, half_words], F32, name="a_split_%d" % z, align_bytes=64)
+            for z in range(2)
+        ]
+        a_turned = [
+            keep.tile([P, half_words], F32, name="a_turned_%d" % z, align_bytes=64)
+            for z in range(2)
+        ]
+
+        def split_blocks(copy, z):
+            copy(
+                out=a_split[z][:].rearrange("p (x u i) -> p x u i", u=2, i=SQUARE),
+                in_=a_blocks[:]
+                .bitcast(F32)[:, z * half_words : (z + 1) * half_words]
+                .rearrange("p (x i u) -> p x u i", u=2, i=SQUARE),
+            )
+
+        def turn_blocks(z):
+            nc.vector.transpose(out=a_turned[z][:], in_=a_split[z][:])
+
+        def join_blocks(copy, z):
+            copy(
+                out=a_grouped[2][:]
+                .bitcast(F32)[:, z * half_words : (z + 1) * half_words]
+                .rearrange("p (x k u) -> p x k u", u=2, k=SQUARE),
+                in_=a_turned[z][:].rearrange("p (x u k) -> p x k u", u=2, k=SQUARE),
+            )
+
         def negate_adjacency(r):
             slot_width = RANGES[r][1] * P * PACK
             nc.vector.tensor_scalar_mul(
@@ -162,11 +205,11 @@ def tile_nconv_pa_t_kernel(tc, x, Ar, Ai, Aj, Ak, out):
                     in_=a_grouped[r][:, PACK * span.start : PACK * span.stop],
                 )
 
-        def multiply(r, g, t, target):
-            columns = RANGES[r][1] * P
+        def multiply(r, first, tiles, g, t, target):
             for a in range(Q):
                 s = slice((t % 2) * P, (t % 2 + 1) * P)
-                n = slice(slot_of(g, a) * columns, (slot_of(g, a) + 1) * columns)
+                start = (slot_of(g, a) * RANGES[r][1] + first) * P
+                n = slice(start, start + tiles * P)
                 nc.tensor.matmul_mx(
                     out=target,
                     lhsT=x_codes[g ^ a, t // 2][:, s].bitcast(FP8X4),
@@ -177,8 +220,7 @@ def tile_nconv_pa_t_kernel(tc, x, Ar, Ai, Aj, Ak, out):
                     stop=(a == Q - 1),
                 )
 
-        def store(r, g, result):
-            first, tiles = RANGES[r]
+        def store(first, tiles, g, result):
             for b in range(B):
                 nc.sync.dma_start(
                     out=out[
@@ -187,10 +229,10 @@ def tile_nconv_pa_t_kernel(tc, x, Ar, Ai, Aj, Ak, out):
                     in_=result[b:P:B, :],
                 )
 
-        def multiply_narrow(r, g, acc, steps):
+        def multiply_narrow(r, i, g, acc, steps):
             for t in steps:
                 k = t % 4
-                multiply(r, g, t, acc[:, k * P : (k + 1) * P])
+                multiply(r, i, 1, g, t, acc[:, k * P : (k + 1) * P])
 
         def unload_narrow(copy, h, acc, result):
             copy(
@@ -202,7 +244,7 @@ def tile_nconv_pa_t_kernel(tc, x, Ar, Ai, Aj, Ak, out):
             acc = psum.tile([P, BANK], F32, tag="bank")
             for t in (2 * w, 2 * w + 1):
                 k = t % 2
-                multiply(r, g, t, acc[:, 2 * k * P : 2 * (k + 1) * P])
+                multiply(r, 0, 2, g, t, acc[:, 2 * k * P : 2 * (k + 1) * P])
             return acc
 
         def permute_wide(h, staged, result):
@@ -242,7 +284,7 @@ def tile_nconv_pa_t_kernel(tc, x, Ar, Ai, Aj, Ak, out):
         accs = [psum.tile([P, BANK], F32, tag="bank", name="acc") for g in range(Q)]
         for t in (0, 1):
             for g in range(Q):
-                multiply_narrow(0, g, accs[g], (t,))
+                multiply_narrow(0, 0, g, accs[g], (t,))
         for g in range(LAST):
             regroup_x(by_scalar, g, 3)
             quantise_x(g, 3)
@@ -253,36 +295,45 @@ def tile_nconv_pa_t_kernel(tc, x, Ar, Ai, Aj, Ak, out):
         quantise_x(LAST, 2)
         quantise_x(LAST, 3)
         for g in range(Q):
-            multiply_narrow(0, g, accs[g], (2, 3))
+            multiply_narrow(0, 0, g, accs[g], (2, 3))
             unload_narrow(by_vector if g % 2 else by_scalar, 0, accs[g], results[g])
-        for i in range(2):
-            transpose_adjacency(1, i, (by_scalar, by_vector))
+        transpose_adjacency(1, 0, (by_scalar, by_vector))
         negate_adjacency(1)
         quantise_adjacency(1)
         accs = [psum.tile([P, BANK], F32, tag="bank", name="acc") for g in range(Q)]
+        split_blocks(by_scalar, 0)
         for g in range(Q):
-            multiply_narrow(0, g, accs[g], (4, 5, 6, 7))
+            multiply_narrow(0, 0, g, accs[g], (4, 5, 6, 7))
             unload_narrow(by_vector if g % 2 else by_scalar, 1, accs[g], results[g])
-            store(0, g, results[g])
+            store(0, 1, g, results[g])
+            if g == 0:
+                split_blocks(by_scalar, 1)
 
-        for g in range(Q):
-            staged = wide.tile([P, 2 * P * T], F32, name="staged")
-            result = wide.tile([P, 2 * P * T], F32, name="result")
-            for w in range(T_PAIRS):
-                acc = multiply_wide(1, g, w)
-                by_scalar(out=staged[:, w * BANK : (w + 1) * BANK], in_=acc[:])
-                if w % 2 == 1:
-                    permute_wide(w // 2, staged, result)
-            store(1, g, result)
-            if g == 1:
-                transpose_adjacency(2, 0, (by_scalar, by_vector))
-                negate_adjacency(2)
-                quantise_adjacency(2)
-
-        for g in range(Q):
+        def narrow_group(r, i, g, copies):
             result = narrow.tile([P, P * T], F32, name="result_%d" % g)
             for h in range(2):
                 acc = psum.tile([P, BANK], F32, tag="bank")
-                multiply_narrow(2, g, acc, range(4 * h, 4 * h + 4))
-                unload_narrow(by_vector if h else by_scalar, h, acc, result)
-            store(2, g, result)
+                multiply_narrow(r, i, g, acc, range(4 * h, 4 * h + 4))
+                unload_narrow(copies[h], h, acc, result)
+            store(RANGES[r][0] + i, 1, g, result)
+
+        for z in range(2):
+            turn_blocks(z)
+        for z in range(2):
+            join_blocks(by_vector, z)
+        negate_adjacency(2)
+        quantise_adjacency(2)
+        for g in range(Q):
+            narrow_group(1, 0, g, (by_scalar, by_scalar))
+
+        for g in range(Q - 1):
+            staged = wide.tile([P, 2 * P * T], F32, name="staged")
+            result = wide.tile([P, 2 * P * T], F32, name="result")
+            for w in range(T_PAIRS):
+                acc = multiply_wide(2, g, w)
+                by_scalar(out=staged[:, w * BANK : (w + 1) * BANK], in_=acc[:])
+                if w % 2 == 1:
+                    permute_wide(w // 2, staged, result)
+            store(2, 2, g, result)
+        for i in range(2):
+            narrow_group(2, i, Q - 1, (by_scalar, by_vector))

@@ -71,21 +71,23 @@ def tile_nconv_pa_t_kernel(tc, x, Ar, Ai, Aj, Ak, out):
                     in_=x[b, g * GROUP : (g + 1) * GROUP].rearrange("c m t -> c (m t)"),
                 )
             x_raw.append(raw)
-        load_adjacency(1)
-        block_width = 2 * N * RANGES[2][1]
-        a_blocks = keep.tile([P, 2 * block_width], BF16, name="a_blocks", align_bytes=64)
-        for a in range(Q):
-            rows = adjacency[a][RANGES[2][0] * P : (RANGES[2][0] + RANGES[2][1]) * P, :]
-            per_part = 2 * block_width // Q
-            for d in range(P // SQUARE):
-                nc.sync.dma_start(
-                    out=a_blocks[
-                        d * SQUARE : (d + 1) * SQUARE, a * per_part : (a + 1) * per_part
-                    ].rearrange("k (f i) -> k f i", i=4 * SQUARE),
-                    in_=rows[:, d * 4 * SQUARE : (d + 1) * 4 * SQUARE].rearrange(
-                        "(f k) i -> k f i", k=SQUARE
-                    ),
-                )
+        a_blocks = {}
+        for r in (1, 2):
+            first, tiles = RANGES[r]
+            part = N * tiles
+            blocks = keep.tile([P, Q * part], BF16, name="a_blocks_%d" % r, align_bytes=64)
+            for a in range(Q):
+                rows = adjacency[a][first * P : (first + tiles) * P, :]
+                for d in range(P // SQUARE):
+                    nc.sync.dma_start(
+                        out=blocks[
+                            d * SQUARE : (d + 1) * SQUARE, a * part : (a + 1) * part
+                        ].rearrange("k (f i) -> k f i", i=4 * SQUARE),
+                        in_=rows[:, d * 4 * SQUARE : (d + 1) * 4 * SQUARE].rearrange(
+                            "(f k) i -> k f i", k=SQUARE
+                        ),
+                    )
+            a_blocks[r] = blocks
 
         step_width = P * PACK
         x_grouped = {}
@@ -158,33 +160,35 @@ def tile_nconv_pa_t_kernel(tc, x, Ar, Ai, Aj, Ak, out):
                     in_=bank[:].rearrange("p (s u n) -> p s n u", s=2, u=2, n=P),
                 )
 
-        half_words = block_width // 2
-        a_split = [
-            keep.tile([P, half_words], F32, name="a_split_%d" % z, align_bytes=64)
-            for z in range(2)
-        ]
-        a_turned = [
-            keep.tile([P, half_words], F32, name="a_turned_%d" % z, align_bytes=64)
-            for z in range(2)
-        ]
+        piece_words = 1024
+        pieces = [(r, z) for r in (1, 2) for z in range(2 * RANGES[r][1] * N // piece_words)]
+        a_split = {}
+        a_turned = {}
+        for r, z in pieces:
+            a_split[r, z] = keep.tile(
+                [P, piece_words], F32, name="a_split_%d_%d" % (r, z), align_bytes=64
+            )
+            a_turned[r, z] = keep.tile(
+                [P, piece_words], F32, name="a_turned_%d_%d" % (r, z), align_bytes=64
+            )
 
-        def split_blocks(copy, z):
+        def split_blocks(copy, r, z):
             copy(
-                out=a_split[z][:].rearrange("p (x u i) -> p x u i", u=2, i=SQUARE),
-                in_=a_blocks[:]
-                .bitcast(F32)[:, z * half_words : (z + 1) * half_words]
+                out=a_split[r, z][:].rearrange("p (x u i) -> p x u i", u=2, i=SQUARE),
+                in_=a_blocks[r][:]
+                .bitcast(F32)[:, z * piece_words : (z + 1) * piece_words]
                 .rearrange("p (x i u) -> p x u i", u=2, i=SQUARE),
             )
 
-        def turn_blocks(z):
-            nc.vector.transpose(out=a_turned[z][:], in_=a_split[z][:])
+        def turn_blocks(r, z):
+            nc.vector.transpose(out=a_turned[r, z][:], in_=a_split[r, z][:])
 
-        def join_blocks(copy, z):
+        def join_blocks(copy, r, z):
             copy(
-                out=a_grouped[2][:]
-                .bitcast(F32)[:, z * half_words : (z + 1) * half_words]
+                out=a_grouped[r][:]
+                .bitcast(F32)[:, z * piece_words : (z + 1) * piece_words]
                 .rearrange("p (x k u) -> p x k u", u=2, k=SQUARE),
-                in_=a_turned[z][:].rearrange("p (x u k) -> p x k u", u=2, k=SQUARE),
+                in_=a_turned[r, z][:].rearrange("p (x u k) -> p x k u", u=2, k=SQUARE),
             )
 
         def negate_adjacency(r):
@@ -205,20 +209,21 @@ def tile_nconv_pa_t_kernel(tc, x, Ar, Ai, Aj, Ak, out):
                     in_=a_grouped[r][:, PACK * span.start : PACK * span.stop],
                 )
 
-        def multiply(r, first, tiles, g, t, target):
-            for a in range(Q):
-                s = slice((t % 2) * P, (t % 2 + 1) * P)
-                start = (slot_of(g, a) * RANGES[r][1] + first) * P
-                n = slice(start, start + tiles * P)
-                nc.tensor.matmul_mx(
-                    out=target,
-                    lhsT=x_codes[g ^ a, t // 2][:, s].bitcast(FP8X4),
-                    lhsT_scale=x_scales[g ^ a, t // 2][:, s],
-                    rhs=a_codes[r][:, n].bitcast(FP8X4),
-                    rhs_scale=a_scales[r][:, n],
-                    start=(a == 0),
-                    stop=(a == Q - 1),
-                )
+        def multiply(r, first, tiles, t, targets):
+            s = slice((t % 2) * P, (t % 2 + 1) * P)
+            for h in range(Q):
+                for g in targets:
+                    start = (slot_of(g, g ^ h) * RANGES[r][1] + first) * P
+                    n = slice(start, start + tiles * P)
+                    nc.tensor.matmul_mx(
+                        out=targets[g],
+                        lhsT=x_codes[h, t // 2][:, s].bitcast(FP8X4),
+                        lhsT_scale=x_scales[h, t // 2][:, s],
+                        rhs=a_codes[r][:, n].bitcast(FP8X4),
+                        rhs_scale=a_scales[r][:, n],
+                        start=(h == 0),
+                        stop=(h == Q - 1),
+                    )
 
         def store(first, tiles, g, result):
             for b in range(B):
@@ -229,10 +234,10 @@ def tile_nconv_pa_t_kernel(tc, x, Ar, Ai, Aj, Ak, out):
                     in_=result[b:P:B, :],
                 )
 
-        def multiply_narrow(r, i, g, acc, steps):
+        def multiply_narrow(r, i, accs, steps):
             for t in steps:
                 k = t % 4
-                multiply(r, i, 1, g, t, acc[:, k * P : (k + 1) * P])
+                multiply(r, i, 1, t, {g: accs[g][:, k * P : (k + 1) * P] for g in accs})
 
         def unload_narrow(copy, h, acc, result):
             copy(
@@ -244,7 +249,7 @@ def tile_nconv_pa_t_kernel(tc, x, Ar, Ai, Aj, Ak, out):
             acc = psum.tile([P, BANK], F32, tag="bank")
             for t in (2 * w, 2 * w + 1):
                 k = t % 2
-                multiply(r, 0, 2, g, t, acc[:, 2 * k * P : 2 * (k + 1) * P])
+                multiply(r, 0, 2, t, {g: acc[:, 2 * k * P : 2 * (k + 1) * P]})
             return acc
 
         def permute_wide(h, staged, result):
@@ -266,65 +271,83 @@ def tile_nconv_pa_t_kernel(tc, x, Ar, Ai, Aj, Ak, out):
             regroup_x(by_scalar, g, 0)
             regroup_x(by_vector, g, 1)
             quantise_x(g, 0)
-            quantise_x(g, 1)
-            regroup_x(by_scalar, g, 2)
-            if g > 0:
-                quantise_x(g - 1, 2)
+            if g < LAST - 1:
+                regroup_x(by_scalar, g, 2)
+            if g == 0:
+                regroup_x(by_vector, g, 3)
         transpose_x(LAST, 0)
         transpose_x(LAST, 1)
         regroup_x(by_scalar, LAST, 0, 0, 1)
         regroup_x(by_scalar, LAST, 0, 1, 1)
+        quantise_x(0, 1)
+        quantise_x(1, 1)
         quantise_x(LAST, 0, 0, 1)
         quantise_x(LAST, 0, 1, 1)
-        regroup_x(by_vector, LAST, 1)
-        quantise_x(LAST, 1)
-        quantise_x(LAST - 1, 2)
+        regroup_x(by_scalar, LAST, 1)
+        regroup_x(by_vector, 1, 3)
+        regroup_x(by_scalar, LAST - 1, 2)
+        quantise_x(2, 1)
+        quantise_x(3, 1)
 
-        results = [narrow.tile([P, P * T], F32, name="result_%d" % g) for g in range(Q)]
-        accs = [psum.tile([P, BANK], F32, tag="bank", name="acc") for g in range(Q)]
-        for t in (0, 1):
-            for g in range(Q):
-                multiply_narrow(0, 0, g, accs[g], (t,))
-        for g in range(LAST):
-            regroup_x(by_scalar, g, 3)
-            quantise_x(g, 3)
+        def four_banks():
+            return {g: psum.tile([P, BANK], F32, tag="bank", name="acc") for g in range(Q)}
+
+        def narrow_results():
+            return [narrow.tile([P, P * T], F32, name="result_%d" % g) for g in range(Q)]
+
+        results = narrow_results()
+        accs = four_banks()
+        multiply_narrow(0, 0, {g: accs[g] for g in range(LAST)}, (0,))
+        multiply_narrow(0, 0, {LAST: accs[LAST]}, (0,))
+        multiply_narrow(0, 0, accs, (1,))
         transpose_x(LAST, 2)
         transpose_x(LAST, 3)
         regroup_x(by_scalar, LAST, 2)
+        for g in range(LAST):
+            quantise_x(g, 2)
         regroup_x(by_vector, LAST, 3)
         quantise_x(LAST, 2)
-        quantise_x(LAST, 3)
+        regroup_x(by_scalar, 2, 3)
+        split_blocks(by_scalar, 1, 0)
+        for g in (0, 1, 3, 2):
+            quantise_x(g, 3)
+        multiply_narrow(0, 0, accs, (2, 3))
         for g in range(Q):
-            multiply_narrow(0, 0, g, accs[g], (2, 3))
-            unload_narrow(by_vector if g % 2 else by_scalar, 0, accs[g], results[g])
-        transpose_adjacency(1, 0, (by_scalar, by_vector))
+            unload_narrow(by_scalar, 0, accs[g], results[g])
+        turn_blocks(1, 0)
+        join_blocks(by_vector, 1, 0)
         negate_adjacency(1)
         quantise_adjacency(1)
-        accs = [psum.tile([P, BANK], F32, tag="bank", name="acc") for g in range(Q)]
-        split_blocks(by_scalar, 0)
+        accs = four_banks()
+        multiply_narrow(0, 0, accs, (4, 5, 6, 7))
+        split_blocks(by_scalar, 2, 0)
         for g in range(Q):
-            multiply_narrow(0, 0, g, accs[g], (4, 5, 6, 7))
             unload_narrow(by_vector if g % 2 else by_scalar, 1, accs[g], results[g])
             store(0, 1, g, results[g])
-            if g == 0:
-                split_blocks(by_scalar, 1)
+        split_blocks(by_scalar, 2, 1)
+
+        for z in range(2):
+            turn_blocks(2, z)
+        for z in range(2):
+            join_blocks(by_vector, 2, z)
+        negate_adjacency(2)
+        quantise_adjacency(2)
+        results = narrow_results()
+        for h in range(2):
+            accs = four_banks()
+            multiply_narrow(1, 0, accs, range(4 * h, 4 * h + 4))
+            for g in range(Q):
+                unload_narrow(by_scalar, h, accs[g], results[g])
+        for g in range(Q):
+            store(1, 1, g, results[g])
 
         def narrow_group(r, i, g, copies):
             result = narrow.tile([P, P * T], F32, name="result_%d" % g)
             for h in range(2):
                 acc = psum.tile([P, BANK], F32, tag="bank")
-                multiply_narrow(r, i, g, acc, range(4 * h, 4 * h + 4))
+                multiply_narrow(r, i, {g: acc}, range(4 * h, 4 * h + 4))
                 unload_narrow(copies[h], h, acc, result)
             store(RANGES[r][0] + i, 1, g, result)
-
-        for z in range(2):
-            turn_blocks(z)
-        for z in range(2):
-            join_blocks(by_vector, z)
-        negate_adjacency(2)
-        quantise_adjacency(2)
-        for g in range(Q):
-            narrow_group(1, 0, g, (by_scalar, by_scalar))
 
         for g in range(Q - 1):
             staged = wide.tile([P, 2 * P * T], F32, name="staged")

@@ -275,8 +275,8 @@ def tile_nconv_pa_t_kernel(tc, x, Ar, Ai, Aj, Ak, out):
                 regroup_x(by_scalar, g, 2)
             if g == 0:
                 regroup_x(by_vector, g, 3)
-        transpose_x(LAST, 0)
-        transpose_x(LAST, 1)
+        for w in range(T_PAIRS):
+            transpose_x(LAST, w)
         regroup_x(by_scalar, LAST, 0, 0, 1)
         regroup_x(by_scalar, LAST, 0, 1, 1)
         quantise_x(0, 1)
@@ -297,29 +297,28 @@ def tile_nconv_pa_t_kernel(tc, x, Ar, Ai, Aj, Ak, out):
 
         results = narrow_results()
         accs = four_banks()
-        multiply_narrow(0, 0, {g: accs[g] for g in range(LAST)}, (0,))
-        multiply_narrow(0, 0, {LAST: accs[LAST]}, (0,))
-        multiply_narrow(0, 0, accs, (1,))
-        transpose_x(LAST, 2)
-        transpose_x(LAST, 3)
+        for g in range(Q):
+            multiply_narrow(0, 0, {g: accs[g]}, (0, 1))
         regroup_x(by_scalar, LAST, 2)
         for g in range(LAST):
             quantise_x(g, 2)
-        regroup_x(by_vector, LAST, 3)
         quantise_x(LAST, 2)
-        regroup_x(by_scalar, 2, 3)
-        split_blocks(by_scalar, 1, 0)
-        for g in (0, 1, 3, 2):
-            quantise_x(g, 3)
-        multiply_narrow(0, 0, accs, (2, 3))
-        for g in range(Q):
-            unload_narrow(by_scalar, 0, accs[g], results[g])
+        split_blocks(by_vector, 1, 0)
         turn_blocks(1, 0)
+        regroup_x(by_scalar, 2, 3)
+        regroup_x(by_scalar, LAST, 3)
+        for g in range(Q):
+            quantise_x(g, 3)
         join_blocks(by_vector, 1, 0)
         negate_adjacency(1)
         quantise_adjacency(1)
+        for g in range(Q):
+            multiply_narrow(0, 0, {g: accs[g]}, (2, 3))
+            unload_narrow(by_scalar, 0, accs[g], results[g])
         accs = four_banks()
-        multiply_narrow(0, 0, accs, (4, 5, 6, 7))
+        for steps in ((4, 5), (6, 7)):
+            for g in range(Q):
+                multiply_narrow(0, 0, {g: accs[g]}, steps)
         split_blocks(by_scalar, 2, 0)
         for g in range(Q):
             unload_narrow(by_vector if g % 2 else by_scalar, 1, accs[g], results[g])

@@ -106,6 +106,13 @@ def tile_nconv_pa_t_kernel(tc, x, Ar, Ai, Aj, Ak, out):
                 )
         x_banks = {}
 
+        def keep_busy(count):
+            for i in range(count):
+                idle = psum.tile([P, BANK], F32, tag="bank", name="idle")
+                nc.tensor.matmul(
+                    idle[:], a_rows[0, 0][:, 0:P], a_rows[0, 1][:], start=True, stop=True
+                )
+
         def transpose_x(g, w):
             words = x_raw[g][:].bitcast(F32).rearrange(
                 "p (q j w) -> p q j w", q=P, j=PACK, w=T_PAIRS
@@ -265,9 +272,12 @@ def tile_nconv_pa_t_kernel(tc, x, Ar, Ai, Aj, Ak, out):
         transpose_adjacency(0, 0, (by_scalar, by_vector))
         negate_adjacency(0)
         quantise_adjacency(0)
+        keep_busy(3)
         for g in range(LAST):
             for w in range(T_PAIRS):
                 transpose_x(g, w)
+                if w % 2 == 1:
+                    keep_busy(1)
             regroup_x(by_scalar, g, 0)
             regroup_x(by_vector, g, 1)
             quantise_x(g, 0)
@@ -277,6 +287,8 @@ def tile_nconv_pa_t_kernel(tc, x, Ar, Ai, Aj, Ak, out):
                 regroup_x(by_vector, g, 3)
         for w in range(T_PAIRS):
             transpose_x(LAST, w)
+            if w == 1:
+                keep_busy(1)
         regroup_x(by_scalar, LAST, 0, 0, 1)
         regroup_x(by_scalar, LAST, 0, 1, 1)
         quantise_x(0, 1)
@@ -302,23 +314,21 @@ def tile_nconv_pa_t_kernel(tc, x, Ar, Ai, Aj, Ak, out):
         regroup_x(by_scalar, LAST, 2)
         for g in range(LAST):
             quantise_x(g, 2)
+        regroup_x(by_vector, LAST, 3)
         quantise_x(LAST, 2)
-        split_blocks(by_vector, 1, 0)
-        turn_blocks(1, 0)
         regroup_x(by_scalar, 2, 3)
-        regroup_x(by_scalar, LAST, 3)
-        for g in range(Q):
+        split_blocks(by_scalar, 1, 0)
+        for g in (0, 1, 3, 2):
             quantise_x(g, 3)
-        join_blocks(by_vector, 1, 0)
-        negate_adjacency(1)
-        quantise_adjacency(1)
         for g in range(Q):
             multiply_narrow(0, 0, {g: accs[g]}, (2, 3))
             unload_narrow(by_scalar, 0, accs[g], results[g])
+        turn_blocks(1, 0)
+        join_blocks(by_vector, 1, 0)
+        negate_adjacency(1)
+        quantise_adjacency(1)
         accs = four_banks()
-        for steps in ((4, 5), (6, 7)):
-            for g in range(Q):
-                multiply_narrow(0, 0, {g: accs[g]}, steps)
+        multiply_narrow(0, 0, accs, (4, 5, 6, 7))
         split_blocks(by_scalar, 2, 0)
         for g in range(Q):
             unload_narrow(by_vector if g % 2 else by_scalar, 1, accs[g], results[g])

from contextlib import ExitStack

import concourse.mybir as mybir
from concourse.masks import make_identity

F32 = mybir.dt.float32
BF16 = mybir.dt.bfloat16
U32 = mybir.dt.uint32
U8 = mybir.dt.uint8
FP8X4 = mybir.dt.float8_e4m3fn_x4

B, C, N, T, Q = 4, 128, 512, 8, 4
P = 128
PACK = 4
GROUP = C // Q
T_PAIRS = T // 2
BANK = 512
PSUM_BANKS = 8
LAST = Q - 1

SIGN = (
    (+1, -1, -1, -1),
    (+1, +1, +1, -1),
    (+1, -1, +1, +1),
    (+1, +1, -1, +1),
)
SLOTS = 2 * Q - 1
SLOT_RUNS = ((0, 4), (4, 2), (6, 1))

RANGES = ((0, 1), (1, 1), (2, 2))
SQUARE = 32

FLOPS = 2 * Q * N * N * B * C * T


def slot_of(g, a):
    return a if SIGN[g][a] > 0 else Q - 1 + a


def tile_nconv_pa_t_kernel(tc, x, Ar, Ai, Aj, Ak, out):
    nc = tc.nc
    adjacency = (Ar, Ai, Aj, Ak)
    by_scalar = nc.scalar.copy
    by_vector = nc.vector.tensor_copy

    with ExitStack() as stack:
        keep = stack.enter_context(tc.tile_pool(name="keep", bufs=1))
        narrow = stack.enter_context(tc.tile_pool(name="narrow", bufs=2))
        wide = stack.enter_context(tc.tile_pool(name="wide", bufs=2))
        psum = stack.enter_context(tc.psum_pool(name="psum", bufs=PSUM_BANKS))
        stack.enter_context(tc.manual_schedule())

        ident = keep.tile([P, P], F32)
        make_identity(nc, ident[:])

        a_rows = {}

        def load_adjacency(nt):
            for a in range(Q):
                rows = keep.tile([P, N], BF16, name="a_rows_%d_%d" % (nt, a))
                nc.sync.dma_start(out=rows[:], in_=adjacency[a][nt * P : (nt + 1) * P, :])
                a_rows[nt, a] = rows

        load_adjacency(0)
        x_raw = []
        for g in range(Q):
            raw = keep.tile([P, N * T], BF16, name="x_raw_%d" % g)
            for b in range(B):
                nc.sync.dma_start(
                    out=raw[b:P:B, :],
                    in_=x[b, g * GROUP : (g + 1) * GROUP].rearrange("c m t -> c (m t)"),
                )
            x_raw.append(raw)
        a_blocks = {}
        for r in (1, 2):
            first, tiles = RANGES[r]
            part = N * tiles
            blocks = keep.tile([P, Q * part], BF16, name="a_blocks_%d" % r, align_bytes=64)
            for a in range(Q):
                rows = adjacency[a][first * P : (first + tiles) * P, :]
                for d in range(P // SQUARE):
                    nc.sync.dma_start(
                        out=blocks[
                            d * SQUARE : (d + 1) * SQUARE, a * part : (a + 1) * part
                        ].rearrange("k (f i) -> k f i", i=4 * SQUARE),
                        in_=rows[:, d * 4 * SQUARE : (d + 1) * 4 * SQUARE].rearrange(
                            "(f k) i -> k f i", k=SQUARE
                        ),
                    )
            a_blocks[r] = blocks

        step_width = P * PACK
        x_grouped = {}
        x_codes = {}
        x_scales = {}
        for g in range(Q):
            for w in range(T_PAIRS):
                x_grouped[g, w] = keep.tile(
                    [P, 2 * step_width], BF16, name="x_grouped_%d_%d" % (g, w), align_bytes=64
                )
                x_codes[g, w] = keep.tile(
                    [P, 2 * P], U32, name="x_codes_%d_%d" % (g, w), align_bytes=64
                )
                x_scales[g, w] = keep.tile(
                    [P, 2 * P], U8, name="x_scales_%d_%d" % (g, w), align_bytes=64
                )
        x_banks = {}

        def keep_busy(count):
            for i in range(count):
                idle = psum.tile([P, BANK], F32, tag="bank", name="idle")
                nc.tensor.matmul(
                    idle[:], a_rows[0, 0][:, 0:P], a_rows[0, 1][:], start=True, stop=True
                )

        def transpose_x(g, w):
            words = x_raw[g][:].bitcast(F32).rearrange(
                "p (q j w) -> p q j w", q=P, j=PACK, w=T_PAIRS
            )
            bank = psum.tile([P, BANK], F32, tag="bank")
            for j in range(PACK):
                nc.tensor.transpose(bank[:, j * P : (j + 1) * P], words[:, :, j, w], ident[:])
            x_banks[g, w] = bank

        def regroup_x(copy, g, w, first=0, steps=2):
            target = x_grouped[g, w][:, first * step_width : (first + steps) * step_width]
            source = x_banks[g, w][:].bitcast(BF16).rearrange(
                "p (j c s) -> p s c j", j=PACK, c=P, s=2
            )
            copy(
                out=target.rearrange("p (s c j) -> p s c j", s=steps, c=P, j=PACK),
                in_=source[:, first : first + steps, :, :],
            )

        def quantise_x(g, w, first=0, steps=2):
            nc.vector.quantize_mx(
                out=x_codes[g, w][:, first * P : (first + steps) * P].bitcast(FP8X4),
                scales=x_scales[g, w][:, first * P : (first + steps) * P],
                in_=x_grouped[g, w][:, first * step_width : (first + steps) * step_width],
            )

        a_grouped = []
        a_codes = []
        a_scales = []
        for r in range(len(RANGES)):
            columns = SLOTS * RANGES[r][1] * P
            a_grouped.append(
                keep.tile([P, PACK * columns], BF16, name="a_grouped_%d" % r, align_bytes=64)
            )
            a_codes.append(keep.tile([P, columns], U32, name="a_codes_%d" % r, align_bytes=64))
            a_scales.append(keep.tile([P, columns], U8, name="a_scales_%d" % r, align_bytes=64))

        def transpose_adjacency(r, i, copies):
            first, tiles = RANGES[r]
            grouped_words = a_grouped[r][:].bitcast(F32).rearrange(
                "p (s i n u) -> p s i n u", s=SLOTS, i=tiles, n=P, u=2
            )
            for pair in range(2):
                bank = psum.tile([P, BANK], F32, tag="bank")
                for k in range(4):
                    words = a_rows[first + i, 2 * pair + k // 2][:].bitcast(F32)
                    nc.tensor.transpose(
                        bank[:, k * P : (k + 1) * P], words[:, k % 2 : 2 * P : 2], ident[:]
                    )
                copies[pair](
                    out=grouped_words[:, 2 * pair : 2 * pair + 2, i, :, :],
                    in_=bank[:].rearrange("p (s u n) -> p s n u", s=2, u=2, n=P),
                )

        piece_words = 1024
        pieces = [(r, z) for r in (1, 2) for z in range(2 * RANGES[r][1] * N // piece_words)]
        a_split = {}
        a_turned = {}
        for r, z in pieces:
            a_split[r, z] = keep.tile(
                [P, piece_words], F32, name="a_split_%d_%d" % (r, z), align_bytes=64
            )
            a_turned[r, z] = keep.tile(
                [P, piece_words], F32, name="a_turned_%d_%d" % (r, z), align_bytes=64
            )

        def split_blocks(copy, r, z):
            copy(
                out=a_split[r, z][:].rearrange("p (x u i) -> p x u i", u=2, i=SQUARE),
                in_=a_blocks[r][:]
                .bitcast(F32)[:, z * piece_words : (z + 1) * piece_words]
                .rearrange("p (x i u) -> p x u i", u=2, i=SQUARE),
            )

        def turn_blocks(r, z):
            nc.vector.transpose(out=a_turned[r, z][:], in_=a_split[r, z][:])

        def join_blocks(copy, r, z):
            copy(
                out=a_grouped[r][:]
                .bitcast(F32)[:, z * piece_words : (z + 1) * piece_words]
                .rearrange("p (x k u) -> p x k u", u=2, k=SQUARE),
                in_=a_turned[r, z][:].rearrange("p (x u k) -> p x k u", u=2, k=SQUARE),
            )

        def negate_adjacency(r):
            slot_width = RANGES[r][1] * P * PACK
            nc.vector.tensor_scalar_mul(
                out=a_grouped[r][:, Q * slot_width : SLOTS * slot_width],
                in0=a_grouped[r][:, slot_width : Q * slot_width],
                scalar1=-1.0,
            )

        def quantise_adjacency(r):
            columns = RANGES[r][1] * P
            for first, count in SLOT_RUNS:
                span = slice(first * columns, (first + count) * columns)
                nc.vector.quantize_mx(
                    out=a_codes[r][:, span].bitcast(FP8X4),
                    scales=a_scales[r][:, span],
                    in_=a_grouped[r][:, PACK * span.start : PACK * span.stop],
                )

        def multiply(r, first, tiles, t, targets):
            s = slice((t % 2) * P, (t % 2 + 1) * P)
            for h in range(Q):
                for g in targets:
                    start = (slot_of(g, g ^ h) * RANGES[r][1] + first) * P
                    n = slice(start, start + tiles * P)
                    nc.tensor.matmul_mx(
                        out=targets[g],
                        lhsT=x_codes[h, t // 2][:, s].bitcast(FP8X4),
                        lhsT_scale=x_scales[h, t // 2][:, s],
                        rhs=a_codes[r][:, n].bitcast(FP8X4),
                        rhs_scale=a_scales[r][:, n],
                        start=(h == 0),
                        stop=(h == Q - 1),
                    )

        def store(first, tiles, g, result):
            for b in range(B):
                nc.sync.dma_start(
                    out=out[
                        b, g * GROUP : (g + 1) * GROUP, first * P : (first + tiles) * P, :
                    ].rearrange("c n t -> c (n t)"),
                    in_=result[b:P:B, :],
                )

        def multiply_narrow(r, i, accs, steps):
            for t in steps:
                k = t % 4
                multiply(r, i, 1, t, {g: accs[g][:, k * P : (k + 1) * P] for g in accs})

        def unload_narrow(copy, h, acc, result):
            copy(
                out=result[:].rearrange("p (n t) -> p n t", n=P, t=T)[:, :, 4 * h : 4 * h + 4],
                in_=acc[:].rearrange("p (t n) -> p n t", t=4, n=P),
            )

        def multiply_wide(r, g, w):
            acc = psum.tile([P, BANK], F32, tag="bank")
            for t in (2 * w, 2 * w + 1):
                k = t % 2
                multiply(r, 0, 2, t, {g: acc[:, 2 * k * P : 2 * (k + 1) * P]})
            return acc

        def permute_wide(h, staged, result):
            nc.vector.tensor_copy(
                out=result[:].rearrange("p (n t) -> p n t", n=2 * P, t=T)[
                    :, :, 4 * h : 4 * h + 4
                ],
                in_=staged[:].rearrange("p (t n) -> p n t", t=T, n=2 * P)[
                    :, :, 4 * h : 4 * h + 4
                ],
            )

        transpose_adjacency(0, 0, (by_scalar, by_vector))
        negate_adjacency(0)
        quantise_adjacency(0)
        keep_busy(3)
        for g in range(LAST):
            for w in range(T_PAIRS):
                transpose_x(g, w)
                if w % 2 == 1:
                    keep_busy(1)
            regroup_x(by_scalar, g, 0)
            regroup_x(by_vector, g, 1)
            quantise_x(g, 0)
            if g < LAST - 1:
                regroup_x(by_scalar, g, 2)
            if g == 0:
                regroup_x(by_vector, g, 3)
        for w in range(T_PAIRS):
            transpose_x(LAST, w)
            if w == 1:
                keep_busy(1)
        regroup_x(by_scalar, LAST, 0, 0, 1)
        regroup_x(by_scalar, LAST, 0, 1, 1)
        quantise_x(0, 1)
        quantise_x(1, 1)
        quantise_x(LAST, 0, 0, 1)
        quantise_x(LAST, 0, 1, 1)
        regroup_x(by_scalar, LAST, 1)
        regroup_x(by_vector, 1, 3)
        regroup_x(by_scalar, LAST - 1, 2)
        quantise_x(2, 1)
        quantise_x(3, 1)

        def four_banks():
            return {g: psum.tile([P, BANK], F32, tag="bank", name="acc") for g in range(Q)}

        def narrow_results():
            return [narrow.tile([P, P * T], F32, name="result_%d" % g) for g in range(Q)]

        results = narrow_results()
        accs = four_banks()
        for g in range(Q):
            multiply_narrow(0, 0, {g: accs[g]}, (0, 1))
        regroup_x(by_scalar, LAST, 2)
        for g in range(LAST):
            quantise_x(g, 2)
        regroup_x(by_vector, LAST, 3)
        quantise_x(LAST, 2)
        regroup_x(by_scalar, 2, 3)
        split_blocks(by_scalar, 1, 0)
        for g in (0, 1, 3, 2):
            quantise_x(g, 3)
        for g in range(Q):
            multiply_narrow(0, 0, {g: accs[g]}, (2, 3))
            unload_narrow(by_scalar, 0, accs[g], results[g])
        turn_blocks(1, 0)
        join_blocks(by_vector, 1, 0)
        negate_adjacency(1)
        quantise_adjacency(1)
        accs = four_banks()
        multiply_narrow(0, 0, accs, (4, 5, 6, 7))
        split_blocks(by_scalar, 2, 0)
        for g in range(Q):
            unload_narrow(by_vector if g % 2 else by_scalar, 1, accs[g], results[g])
            store(0, 1, g, results[g])
        split_blocks(by_scalar, 2, 1)

        for z in range(2):
            turn_blocks(2, z)
        for z in range(2):
            join_blocks(by_vector, 2, z)
        negate_adjacency(2)
        quantise_adjacency(2)
        results = narrow_results()
        for h in range(2):
            accs = four_banks()
            multiply_narrow(1, 0, accs, range(4 * h, 4 * h + 4))
            for g in range(Q):
                unload_narrow(by_scalar, h, accs[g], results[g])
        for g in range(Q):
            store(1, 1, g, results[g])

        def narrow_group(r, i, g, copies):
            result = narrow.tile([P, P * T], F32, name="result_%d" % g)
            for h in range(2):
                acc = psum.tile([P, BANK], F32, tag="bank")
                multiply_narrow(r, i, {g: acc}, range(4 * h, 4 * h + 4))
                unload_narrow(copies[h], h, acc, result)
            store(RANGES[r][0] + i, 1, g, result)

        for g in range(Q - 1):
            staged = wide.tile([P, 2 * P * T], F32, name="staged")
            result = wide.tile([P, 2 * P * T], F32, name="result")
            for w in range(T_PAIRS):
                acc = multiply_wide(2, g, w)
                by_scalar(out=staged[:, w * BANK : (w + 1) * BANK], in_=acc[:])
                if w % 2 == 1:
                    permute_wide(w // 2, staged, result)
            store(2, 2, g, result)
        for i in range(2):
            narrow_group(2, i, Q - 1, (by_scalar, by_vector))
